import numpy as np
import ml_dtypes


def mxq(x, axis, fmt="e4m3"):
    dtype, down = {"e4m3": (ml_dtypes.float8_e4m3fn, 7), "e5m2": (ml_dtypes.float8_e5m2, 14)}[fmt]
    v = np.moveaxis(np.asarray(x, np.float32).astype(ml_dtypes.bfloat16).astype(np.float64), axis, -1)
    blocks = v.reshape(v.shape[:-1] + (-1, 32))
    amax = np.abs(blocks).max(-1, keepdims=True)
    byte = np.maximum(np.where(amax > 0, np.frexp(amax)[1] - 1 + 127, 0) - down, 1)
    scale = np.exp2(byte - 127.0)
    codes = (blocks / scale).astype(np.float32).astype(dtype).astype(np.float64)
    return np.moveaxis((codes * scale).reshape(v.shape), -1, axis)


WIDE = False


def mx_kscale(k):
    if not WIDE:
        return np.ones(k)
    levels = np.array([10, -10, 5, -5, 0])
    a = np.random.permutation(np.resize(levels, k // 512 * 4)).reshape(k // 512, 4)
    idx = np.arange(k)
    return np.exp2(a[idx // 512, idx % 128 // 32])


BF16 = ml_dtypes.bfloat16


def bf(x):
    return np.asarray(x, np.float32).astype(BF16)


def f64(x):
    return np.asarray(x).astype(np.float64)


E2M1 = np.array([0.0, 0.5, 1.0, 1.5, 2.0, 3.0, 4.0, 6.0, -0.0, -0.5, -1.0, -1.5, -2.0, -3.0, -4.0, -6.0])


def pack_weight(w, fmt):
    k, n = w.shape
    w = f64(bf(w)).reshape(k // 32, 32, n)
    amax = np.abs(w).max(1)
    if fmt == "e4m3":
        byte = np.frexp(amax)[1] - 1 + 127 - 7
    else:
        mant, ex = np.frexp(amax / 6.0)
        byte = np.where(mant > 0.5, ex, ex - 1) + 127
    byte = np.clip(np.where(amax > 0, byte, 1), 1, 254)
    scaled = (w * np.exp2(127.0 - byte)[:, None, :]).reshape(k, n).astype(np.float32)
    by_word = np.ascontiguousarray(scaled.reshape(k // 512, 128, 4, n).transpose(0, 1, 3, 2))
    if fmt == "e4m3":
        words = by_word.astype(ml_dtypes.float8_e4m3fn).view(np.uint8)
    else:
        c = by_word.astype(ml_dtypes.float4_e2m1fn).view(np.uint8) & 0xF
        words = c[..., 0::2] | (c[..., 1::2] << 4)
    return np.ascontiguousarray(words), np.ascontiguousarray(byte.astype(np.uint8).reshape(k // 512, 16, n))


def unpack_weight(words, scales, fmt):
    g, p, n, _ = words.shape
    if fmt == "e4m3":
        vals = np.ascontiguousarray(words).view(ml_dtypes.float8_e4m3fn).astype(np.float64)
    else:
        nib = np.empty((g, p, n, 4), np.uint8)
        nib[..., 0::2] = words & 0xF
        nib[..., 1::2] = words >> 4
        vals = E2M1[nib]
    vals = vals * np.repeat(np.exp2(scales.astype(np.float64) - 127.0), 8, axis=1)[..., None]
    return vals.transpose(0, 1, 3, 2).reshape(g * 512, n)

def pack4(w):
    words, scales = pack_weight(w, "e2m1")
    return words.reshape(words.shape[0], 128, -1), scales


def unpack4(words, scales):
    return unpack_weight(words.reshape(words.shape[0], 128, -1, 2), scales, "e2m1")


B, L, DIM, H, D = 2, 64, 8192, 16, 64
EPS = 1e-6
THETA = 10000.0


def rope_table(seq_len, head_dim):
    pos = np.arange(seq_len, dtype=np.float64)
    inv = 1.0 / (THETA ** (np.arange(0, head_dim, 2, dtype=np.float64) / head_dim))
    ang = pos[:, None] * inv[None, :]
    cos, sin = np.cos(ang), np.sin(ang)
    rot = np.stack([np.stack([cos, -sin], -1), np.stack([sin, cos], -1)], -2)
    return rot[None, None]


def rms_norm(u, gain):
    rrms = 1.0 / np.sqrt(np.mean(np.square(u), axis=-1, keepdims=True) + EPS)
    return u * rrms * gain


def rope(u, table):
    ur = u.reshape(*u.shape[:-1], -1, 1, 2)
    out = table[..., 0] * ur[..., 0] + table[..., 1] * ur[..., 1]
    return out.reshape(u.shape)


def setup_inputs():
    s = mx_kscale(DIM)
    x = bf(np.random.standard_normal((B, L, DIM)) * s)
    pe = bf(rope_table(L, D))
    words, scales = pack4(np.random.standard_normal((DIM, 3 * H * D)) / np.sqrt(DIM) / s[:, None])
    qkv_b = bf(np.random.standard_normal(3 * H * D) * 0.2)
    q_scale = bf(1.0 + 0.1 * np.random.standard_normal(D))
    k_scale = bf(1.0 + 0.1 * np.random.standard_normal(D))
    return {"x": x,
            "pe": pe,
            "qkv_w_words": words,
            "qkv_w_scales": scales,
            "qkv_b": qkv_b,
            "q_scale": q_scale,
            "k_scale": k_scale}


def reference(x, pe, qkv_w_words, qkv_w_scales, qkv_b, q_scale, k_scale):
    qkv = (mxq(f64(x), 2, "e4m3") @ unpack4(qkv_w_words, qkv_w_scales)) + f64(qkv_b)
    qkv = qkv.reshape(B, L, 3, H, D).transpose(2, 0, 3, 1, 4)
    q, k, v = qkv[0], qkv[1], qkv[2]
    q = rms_norm(q, f64(q_scale))
    k = rms_norm(k, f64(k_scale))
    table = f64(pe)
    return rope(q, table), rope(k, table), v

@@ -1,0 +1,275 @@
+from contextlib import ExitStack
+
+import concourse.mybir as mybir
+from concourse.masks import make_identity
+
+F32 = mybir.dt.float32
+BF16 = mybir.dt.bfloat16
+I32 = mybir.dt.int32
+U8 = mybir.dt.uint8
+U32 = mybir.dt.uint32
+FP8X4 = mybir.dt.float8_e4m3fn_x4
+FP4X4 = mybir.dt.float4_e2m1fn_x4
+ALU = mybir.AluOpType
+ACT = mybir.ActivationFunctionType
+
+P = 128
+BATCH = 2
+POSITIONS = 64
+K = 8192
+K_PASS = 512
+PASSES = K // K_PASS
+HEADS = 16
+FEATURES = 64
+PAIRS = FEATURES // 2
+STREAM = HEADS * FEATURES
+BANK = 512
+HEADS_PER_BANK = BANK // FEATURES
+EPS = 1e-6
+
+QK_COLS = 2 * STREAM
+V_COLS = STREAM
+BIAS_ROWS = (QK_COLS + V_COLS) // BANK
+GAIN_ROW = BIAS_ROWS
+
+X_CHUNKS = 4
+PASSES_PER_CHUNK = PASSES // X_CHUNKS
+SCALE_PASSES_PER_DMA = 4
+
+FLOPS = 2 * P * K * (QK_COLS + V_COLS)
+
+
+def load_weight_scales(nc, planes, qkv_w_scales, first_col, cols):
+    for first_pass in range(0, PASSES, SCALE_PASSES_PER_DMA):
+        some = slice(first_pass, first_pass + SCALE_PASSES_PER_DMA)
+        nc.vector.memset(planes[:, some, :].bitcast(I32), 0)
+        for q in range(8):
+            partition = 32 * (q // 4) + q % 4
+            nc.sync.dma_start(
+                out=planes[partition:P:64, some, :].bitcast(I32),
+                in_=qkv_w_scales[some, q:16:8, first_col : first_col + cols]
+                .rearrange("g q n -> q g n")
+                .bitcast(I32),
+            )
+
+
+def load_weight_words(nc, words, qkv_w_words, first_col, cols):
+    for g in range(PASSES):
+        nc.sync.dma_start(
+            out=words[g][:].bitcast(I32),
+            in_=qkv_w_words[g, :, 2 * first_col : 2 * (first_col + cols)].bitcast(I32),
+        )
+
+
+def multiply(nc, accs, x_codes, x_scales, words, planes):
+    for g in range(PASSES):
+        tokens = slice(g * P, (g + 1) * P)
+        for j in range(len(accs)):
+            nc.tensor.matmul_mx(
+                out=accs[j][:],
+                lhsT=x_codes[:, tokens].bitcast(FP8X4),
+                lhsT_scale=x_scales[:, tokens],
+                rhs=words[g][:, 2 * BANK * j : 2 * BANK * (j + 1)].bitcast(FP4X4),
+                rhs_scale=planes[:, g, BANK * j : BANK * (j + 1)],
+                start=(g == 0),
+                stop=(g == PASSES - 1),
+            )
+
+
+def tile_selfattention_pa_k_kernel(
+    tc, x, pe, qkv_w_words, qkv_w_scales, qkv_b, q_scale, k_scale, out_0, out_1, out_2
+):
+    nc = tc.nc
+    with ExitStack() as ctx:
+        keep = ctx.enter_context(tc.tile_pool(name="keep", bufs=1))
+        stage = ctx.enter_context(tc.tile_pool(name="stage", bufs=2))
+        psum_acc = ctx.enter_context(tc.psum_pool(name="psum_acc", bufs=1))
+        psum_tmp = ctx.enter_context(tc.psum_pool(name="psum_tmp", bufs=2))
+
+        ident_f32 = keep.tile([P, P], F32)
+        make_identity(nc, ident_f32[:])
+        ident_bf16 = keep.tile([P, P], BF16)
+        make_identity(nc, ident_bf16[:])
+
+        warm = keep.tile([P, 1], F32)
+        nc.vector.memset(warm[:], 1.0)
+        nc.scalar.sqrt(warm[:], warm[:])
+        eps = keep.tile([P, 1], F32)
+        nc.vector.memset(eps[:], EPS)
+
+        vectors = keep.tile([P, BANK], BF16)
+        nc.vector.memset(vectors[:], 0.0)
+        nc.scalar.dma_start(out=vectors[0:BIAS_ROWS, :], in_=qkv_b.rearrange("(j n) -> j n", n=BANK))
+        nc.scalar.dma_start(out=vectors[GAIN_ROW : GAIN_ROW + 1, 0:FEATURES], in_=q_scale.unsqueeze(0))
+        nc.scalar.dma_start(
+            out=vectors[GAIN_ROW : GAIN_ROW + 1, FEATURES : 2 * FEATURES], in_=k_scale.unsqueeze(0)
+        )
+        pe_sb = keep.tile([P, PAIRS, 2, 2], BF16)
+        for b in range(BATCH):
+            nc.scalar.dma_start(
+                out=pe_sb[b * POSITIONS : (b + 1) * POSITIONS],
+                in_=pe.rearrange("a b l i r c -> (a b l) i r c"),
+            )
+
+        x_flat = x.rearrange("b l k -> (b l) k")
+        x_cols = K // X_CHUNKS
+        x_sb = []
+        for chunk in range(X_CHUNKS):
+            x_sb.append(keep.tile([P, x_cols], BF16, name="x_sb%d" % chunk))
+            nc.sync.dma_start(out=x_sb[chunk][:], in_=x_flat[:, chunk * x_cols : (chunk + 1) * x_cols])
+
+        planes_qk = keep.tile([P, PASSES, QK_COLS], U8, align_bytes=64)
+        words_qk = [keep.tile([P, 2 * QK_COLS], U8, name="words_qk%d" % g, align_bytes=64) for g in range(PASSES)]
+        load_weight_scales(nc, planes_qk, qkv_w_scales, 0, QK_COLS)
+        load_weight_words(nc, words_qk, qkv_w_words, 0, QK_COLS)
+
+        planes_v = keep.tile([P, PASSES, V_COLS], U8, align_bytes=64)
+        words_v = [keep.tile([P, 2 * V_COLS], U8, name="words_v%d" % g, align_bytes=64) for g in range(PASSES)]
+        load_weight_scales(nc, planes_v, qkv_w_scales, QK_COLS, V_COLS)
+        load_weight_words(nc, words_v, qkv_w_words, QK_COLS, V_COLS)
+
+        bias_qk = keep.tile([P, 2, 2, HEADS, PAIRS], BF16)
+        bias_v = keep.tile([P, V_COLS], BF16)
+        for j in range(BIAS_ROWS):
+            spread = psum_tmp.tile([P, BANK], F32, tag="tmp")
+            nc.tensor.matmul(
+                out=spread[:],
+                lhsT=ident_bf16[:, j : j + 1].to_broadcast([P, P]),
+                rhs=vectors[:],
+                start=True,
+                stop=True,
+            )
+            if j < QK_COLS // BANK:
+                stream = j // 2
+                heads = slice((j % 2) * HEADS_PER_BANK, (j % 2 + 1) * HEADS_PER_BANK)
+                nc.scalar.copy(
+                    out=bias_qk[:, stream, :, heads, :],
+                    in_=spread[:].rearrange("p (h i c) -> p c h i", i=PAIRS, c=2),
+                )
+            else:
+                first = j * BANK - QK_COLS
+                nc.scalar.copy(out=bias_v[:, first : first + BANK], in_=spread[:])
+
+        gains = psum_tmp.tile([P, BANK], F32, tag="tmp")
+        nc.tensor.matmul(
+            out=gains[:],
+            lhsT=ident_bf16[:, GAIN_ROW : GAIN_ROW + 1].to_broadcast([P, P]),
+            rhs=vectors[:],
+            start=True,
+            stop=True,
+        )
+        gain = gains[:, 0 : 2 * FEATURES].rearrange("p (s i c) -> p s i c", s=2, c=2)
+
+        coef_same = keep.tile([P, 2, 2, PAIRS], F32)
+        coef_other = keep.tile([P, 2, 2, PAIRS], F32)
+        for r in range(2):
+            nc.vector.tensor_tensor(
+                out=coef_same[:, :, r, :],
+                in0=gain[:, :, :, r],
+                in1=pe_sb[:, :, r, r].unsqueeze(1).to_broadcast([P, 2, PAIRS]),
+                op=ALU.mult,
+            )
+            nc.vector.tensor_tensor(
+                out=coef_other[:, :, r, :],
+                in0=gain[:, :, :, 1 - r],
+                in1=pe_sb[:, :, r, 1 - r].unsqueeze(1).to_broadcast([P, 2, PAIRS]),
+                op=ALU.mult,
+            )
+
+        x_codes = keep.tile([P, PASSES * P], U32, align_bytes=64)
+        x_scales = keep.tile([P, PASSES * P], U8, align_bytes=64)
+        for chunk in range(X_CHUNKS):
+            x_words = x_sb[chunk][:].bitcast(F32)
+            grouped = stage.tile([P, PASSES_PER_CHUNK, P, 4], BF16, align_bytes=64)
+            for first in range(0, PASSES_PER_CHUNK, 2):
+                turned = psum_tmp.tile([P, 2, 2, P], F32, tag="tmp")
+                for g in range(2):
+                    for u in range(2):
+                        start_col = (K_PASS // 2) * (first + g)
+                        nc.tensor.transpose(
+                            turned[:, g, u, :],
+                            x_words[:, start_col + u : start_col + K_PASS // 2 : 2],
+                            ident_f32[:],
+                        )
+                nc.scalar.copy(
+                    out=grouped[:, first : first + 2, :, :].bitcast(F32),
+                    in_=turned[:].rearrange("p g u m -> p g m u"),
+                )
+            done = slice(chunk * PASSES_PER_CHUNK * P, (chunk + 1) * PASSES_PER_CHUNK * P)
+            nc.vector.quantize_mx(
+                out=x_codes[:, done].bitcast(FP8X4),
+                scales=x_scales[:, done],
+                in_=grouped[:].rearrange("p g m t -> p (g m t)"),
+            )
+
+        acc_qk = [psum_acc.tile([P, BANK], F32, name="acc_qk%d" % j) for j in range(QK_COLS // BANK)]
+        multiply(nc, acc_qk, x_codes, x_scales, words_qk, planes_qk)
+
+        for stream, out_dram in enumerate((out_0, out_1)):
+            y = stage.tile([P, 2, HEADS, PAIRS], F32)
+            for half in range(2):
+                heads = slice(half * HEADS_PER_BANK, (half + 1) * HEADS_PER_BANK)
+                nc.vector.tensor_tensor(
+                    out=y[:, :, heads, :],
+                    in0=acc_qk[2 * stream + half][:].rearrange("p (h i c) -> p c h i", i=PAIRS, c=2),
+                    in1=bias_qk[:, stream, :, heads, :],
+                    op=ALU.add,
+                )
+
+            squares = stage.tile([P, 2, HEADS, PAIRS], F32, bufs=1)
+            nc.scalar.square(squares[:], y[:])
+            sum_squares = stage.tile([P, HEADS], F32)
+            nc.vector.tensor_reduce(
+                out=sum_squares[:],
+                in_=squares[:].rearrange("p c h i -> p h c i"),
+                axis=mybir.AxisListType.XY,
+                op=ALU.add,
+            )
+            rms = stage.tile([P, HEADS], F32)
+            nc.scalar.activation(out=rms[:], in_=sum_squares[:], func=ACT.Sqrt, bias=eps[:], scale=1.0 / FEATURES)
+            inv_rms = stage.tile([P, HEADS], F32)
+            nc.vector.reciprocal(inv_rms[:], rms[:])
+
+            turned_y = stage.tile([P, 2, HEADS, PAIRS], F32)
+            nc.vector.tensor_tensor(
+                out=turned_y[:],
+                in0=y[:],
+                in1=coef_same[:, stream, :, :].unsqueeze(2).to_broadcast([P, 2, HEADS, PAIRS]),
+                op=ALU.mult,
+            )
+            partner = stage.tile([P, 2, HEADS, PAIRS], F32, bufs=1)
+            for r in range(2):
+                nc.vector.tensor_tensor(
+                    out=partner[:, r, :, :],
+                    in0=y[:, 1 - r, :, :],
+                    in1=coef_other[:, stream, r, :].unsqueeze(1).to_broadcast([P, HEADS, PAIRS]),
+                    op=ALU.mult,
+                )
+            nc.vector.tensor_tensor(out=turned_y[:], in0=turned_y[:], in1=partner[:], op=ALU.add)
+
+            result = stage.tile([P, HEADS, PAIRS, 2], F32, bufs=3)
+            nc.vector.tensor_tensor(
+                out=result[:],
+                in0=turned_y[:].rearrange("p r h i -> p h i r"),
+                in1=inv_rms[:].unsqueeze(2).unsqueeze(3).to_broadcast([P, HEADS, PAIRS, 2]),
+                op=ALU.mult,
+            )
+            for b in range(BATCH):
+                nc.sync.dma_start(
+                    out=out_dram[b].rearrange("h l d -> l h d"),
+                    in_=result[b * POSITIONS : (b + 1) * POSITIONS].rearrange("p h i r -> p h (i r)"),
+                )
+
+        acc_v = [psum_acc.tile([P, BANK], F32, name="acc_v%d" % j) for j in range(V_COLS // BANK)]
+        multiply(nc, acc_v, x_codes, x_scales, words_v, planes_v)
+
+        result = stage.tile([P, HEADS, PAIRS, 2], F32, bufs=3)
+        result_v = result[:].rearrange("p h i r -> p (h i r)")
+        for j in range(len(acc_v)):
+            cols = slice(j * BANK, (j + 1) * BANK)
+            nc.vector.tensor_tensor(out=result_v[:, cols], in0=acc_v[j][:], in1=bias_v[:, cols], op=ALU.add)
+        for b in range(BATCH):
+            nc.sync.dma_start(
+                out=out_2[b].rearrange("h l d -> l h d"),
+                in_=result[b * POSITIONS : (b + 1) * POSITIONS].rearrange("p h i r -> p h (i r)"),
+            )

@@ -27,19 +27,21 @@ BANK = 512
 HEADS_PER_BANK = BANK // FEATURES
 EPS = 1e-6
 
-QK_COLS = 2 * STREAM
-V_COLS = STREAM
-BIAS_ROWS = (QK_COLS + V_COLS) // BANK
+STREAMS = 3
+COLS = STREAMS * STREAM
+BANKS_PER_STREAM = STREAM // BANK
+BIAS_ROWS = COLS // BANK
 GAIN_ROW = BIAS_ROWS
 
 X_CHUNKS = 4
 PASSES_PER_CHUNK = PASSES // X_CHUNKS
 SCALE_PASSES_PER_DMA = 4
+WORD_PASSES_PER_DMA = 2
 
-FLOPS = 2 * P * K * (QK_COLS + V_COLS)
+FLOPS = 2 * P * K * COLS
 
 
-def load_weight_scales(nc, planes, qkv_w_scales, first_col, cols):
+def load_weight_scales(nc, planes, qkv_w_scales):
     for first_pass in range(0, PASSES, SCALE_PASSES_PER_DMA):
         some = slice(first_pass, first_pass + SCALE_PASSES_PER_DMA)
         nc.vector.memset(planes[:, some, :].bitcast(I32), 0)
@@ -47,30 +49,34 @@ def load_weight_scales(nc, planes, qkv_w_scales, first_col, cols):
             partition = 32 * (q // 4) + q % 4
             nc.sync.dma_start(
                 out=planes[partition:P:64, some, :].bitcast(I32),
-                in_=qkv_w_scales[some, q:16:8, first_col : first_col + cols]
-                .rearrange("g q n -> q g n")
-                .bitcast(I32),
+                in_=qkv_w_scales[some, q:16:8, :].rearrange("g q n -> q g n").bitcast(I32),
             )
 
 
-def load_weight_words(nc, words, qkv_w_words, first_col, cols):
-    for g in range(PASSES):
+def load_weight_words(nc, words, qkv_w_words, stream):
+    some_bytes = slice(2 * STREAM * stream, 2 * STREAM * (stream + 1))
+    for n, first_pass in enumerate(range(0, PASSES, WORD_PASSES_PER_DMA)):
         nc.sync.dma_start(
-            out=words[g][:].bitcast(I32),
-            in_=qkv_w_words[g, :, 2 * first_col : 2 * (first_col + cols)].bitcast(I32),
+            out=words[n][:].bitcast(I32),
+            in_=qkv_w_words[first_pass : first_pass + WORD_PASSES_PER_DMA, :, some_bytes]
+            .rearrange("g p c -> p g c")
+            .bitcast(I32),
         )
 
 
-def multiply(nc, accs, x_codes, x_scales, words, planes):
+def multiply(nc, accs, x_codes, x_scales, words, planes, stream):
     for g in range(PASSES):
         tokens = slice(g * P, (g + 1) * P)
-        for j in range(len(accs)):
+        for j in range(BANKS_PER_STREAM):
+            first_col = STREAM * stream + BANK * j
             nc.tensor.matmul_mx(
                 out=accs[j][:],
                 lhsT=x_codes[:, tokens].bitcast(FP8X4),
                 lhsT_scale=x_scales[:, tokens],
-                rhs=words[g][:, 2 * BANK * j : 2 * BANK * (j + 1)].bitcast(FP4X4),
-                rhs_scale=planes[:, g, BANK * j : BANK * (j + 1)],
+                rhs=words[g // WORD_PASSES_PER_DMA][
+                    :, g % WORD_PASSES_PER_DMA, 2 * BANK * j : 2 * BANK * (j + 1)
+                ].bitcast(FP4X4),
+                rhs_scale=planes[:, g, first_col : first_col + BANK],
                 start=(g == 0),
                 stop=(g == PASSES - 1),
             )
@@ -118,18 +124,22 @@ def tile_selfattention_pa_k_kernel(
             x_sb.append(keep.tile([P, x_cols], BF16, name="x_sb%d" % chunk))
             nc.sync.dma_start(out=x_sb[chunk][:], in_=x_flat[:, chunk * x_cols : (chunk + 1) * x_cols])
 
-        planes_qk = keep.tile([P, PASSES, QK_COLS], U8, align_bytes=64)
-        words_qk = [keep.tile([P, 2 * QK_COLS], U8, name="words_qk%d" % g, align_bytes=64) for g in range(PASSES)]
-        load_weight_scales(nc, planes_qk, qkv_w_scales, 0, QK_COLS)
-        load_weight_words(nc, words_qk, qkv_w_words, 0, QK_COLS)
-
-        planes_v = keep.tile([P, PASSES, V_COLS], U8, align_bytes=64)
-        words_v = [keep.tile([P, 2 * V_COLS], U8, name="words_v%d" % g, align_bytes=64) for g in range(PASSES)]
-        load_weight_scales(nc, planes_v, qkv_w_scales, QK_COLS, V_COLS)
-        load_weight_words(nc, words_v, qkv_w_words, QK_COLS, V_COLS)
+        planes = keep.tile([P, PASSES, COLS], U8, align_bytes=64)
+        load_weight_scales(nc, planes, qkv_w_scales)
+        words = []
+        for stream in range(STREAMS):
+            words.append(
+                [
+                    keep.tile(
+                        [P, WORD_PASSES_PER_DMA, 2 * STREAM], U8, name="words%d_%d" % (stream, n), align_bytes=64
+                    )
+                    for n in range(PASSES // WORD_PASSES_PER_DMA)
+                ]
+            )
+            load_weight_words(nc, words[stream], qkv_w_words, stream)
 
         bias_qk = keep.tile([P, 2, 2, HEADS, PAIRS], BF16)
-        bias_v = keep.tile([P, V_COLS], BF16)
+        bias_v = keep.tile([P, STREAM], BF16)
         for j in range(BIAS_ROWS):
             spread = psum_tmp.tile([P, BANK], F32, tag="tmp")
             nc.tensor.matmul(
@@ -139,16 +149,16 @@ def tile_selfattention_pa_k_kernel(
                 start=True,
                 stop=True,
             )
-            if j < QK_COLS // BANK:
-                stream = j // 2
-                heads = slice((j % 2) * HEADS_PER_BANK, (j % 2 + 1) * HEADS_PER_BANK)
+            stream = j // BANKS_PER_STREAM
+            half = j % BANKS_PER_STREAM
+            if stream < 2:
+                heads = slice(half * HEADS_PER_BANK, (half + 1) * HEADS_PER_BANK)
                 nc.scalar.copy(
                     out=bias_qk[:, stream, :, heads, :],
                     in_=spread[:].rearrange("p (h i c) -> p c h i", i=PAIRS, c=2),
                 )
             else:
-                first = j * BANK - QK_COLS
-                nc.scalar.copy(out=bias_v[:, first : first + BANK], in_=spread[:])
+                nc.scalar.copy(out=bias_v[:, half * BANK : (half + 1) * BANK], in_=spread[:])
 
         gains = psum_tmp.tile([P, BANK], F32, tag="tmp")
         nc.tensor.matmul(
@@ -202,16 +212,16 @@ def tile_selfattention_pa_k_kernel(
                 in_=grouped[:].rearrange("p g m t -> p (g m t)"),
             )
 
-        acc_qk = [psum_acc.tile([P, BANK], F32, name="acc_qk%d" % j) for j in range(QK_COLS // BANK)]
-        multiply(nc, acc_qk, x_codes, x_scales, words_qk, planes_qk)
-
         for stream, out_dram in enumerate((out_0, out_1)):
+            acc = [psum_acc.tile([P, BANK], F32, name="acc%d_%d" % (stream, j)) for j in range(BANKS_PER_STREAM)]
+            multiply(nc, acc, x_codes, x_scales, words[stream], planes, stream)
+
             y = stage.tile([P, 2, HEADS, PAIRS], F32)
-            for half in range(2):
+            for half in range(BANKS_PER_STREAM):
                 heads = slice(half * HEADS_PER_BANK, (half + 1) * HEADS_PER_BANK)
                 nc.vector.tensor_tensor(
                     out=y[:, :, heads, :],
-                    in0=acc_qk[2 * stream + half][:].rearrange("p (h i c) -> p c h i", i=PAIRS, c=2),
+                    in0=acc[half][:].rearrange("p (h i c) -> p c h i", i=PAIRS, c=2),
                     in1=bias_qk[:, stream, :, heads, :],
                     op=ALU.add,
                 )
@@ -260,12 +270,12 @@ def tile_selfattention_pa_k_kernel(
                     in_=result[b * POSITIONS : (b + 1) * POSITIONS].rearrange("p h i r -> p h (i r)"),
                 )
 
-        acc_v = [psum_acc.tile([P, BANK], F32, name="acc_v%d" % j) for j in range(V_COLS // BANK)]
-        multiply(nc, acc_v, x_codes, x_scales, words_v, planes_v)
+        acc_v = [psum_acc.tile([P, BANK], F32, name="acc_v%d" % j) for j in range(BANKS_PER_STREAM)]
+        multiply(nc, acc_v, x_codes, x_scales, words[2], planes, 2)
 
         result = stage.tile([P, HEADS, PAIRS, 2], F32, bufs=3)
         result_v = result[:].rearrange("p h i r -> p (h i r)")
-        for j in range(len(acc_v)):
+        for j in range(BANKS_PER_STREAM):
             cols = slice(j * BANK, (j + 1) * BANK)
             nc.vector.tensor_tensor(out=result_v[:, cols], in0=acc_v[j][:], in1=bias_v[:, cols], op=ALU.add)
         for b in range(BATCH):

@@ -15,7 +15,6 @@ ACT = mybir.ActivationFunctionType
 
 P = 128
 BATCH = 2
-POSITIONS = 64
 K = 8192
 K_PASS = 512
 PASSES = K // K_PASS
@@ -112,17 +111,16 @@ def tile_selfattention_pa_k_kernel(
         )
         pe_sb = keep.tile([P, PAIRS, 2, 2], BF16)
         for b in range(BATCH):
-            nc.scalar.dma_start(
-                out=pe_sb[b * POSITIONS : (b + 1) * POSITIONS],
-                in_=pe.rearrange("a b l i r c -> (a b l) i r c"),
-            )
+            nc.scalar.dma_start(out=pe_sb[b:P:BATCH], in_=pe.rearrange("a b l i r c -> (a b l) i r c"))
 
-        x_flat = x.rearrange("b l k -> (b l) k")
         x_cols = K // X_CHUNKS
         x_sb = []
         for chunk in range(X_CHUNKS):
             x_sb.append(keep.tile([P, x_cols], BF16, name="x_sb%d" % chunk))
-            nc.sync.dma_start(out=x_sb[chunk][:], in_=x_flat[:, chunk * x_cols : (chunk + 1) * x_cols])
+            for b in range(BATCH):
+                nc.sync.dma_start(
+                    out=x_sb[chunk][b:P:BATCH, :], in_=x[b, :, chunk * x_cols : (chunk + 1) * x_cols]
+                )
 
         planes = keep.tile([P, PASSES, COLS], U8, align_bytes=64)
         load_weight_scales(nc, planes, qkv_w_scales)
@@ -267,7 +265,7 @@ def tile_selfattention_pa_k_kernel(
             for b in range(BATCH):
                 nc.sync.dma_start(
                     out=out_dram[b].rearrange("h l d -> l h d"),
-                    in_=result[b * POSITIONS : (b + 1) * POSITIONS].rearrange("p h i r -> p h (i r)"),
+                    in_=result[b:P:BATCH].rearrange("p h i r -> p h (i r)"),
                 )
 
         acc_v = [psum_acc.tile([P, BANK], F32, name="acc_v%d" % j) for j in range(BANKS_PER_STREAM)]
@@ -281,5 +279,5 @@ def tile_selfattention_pa_k_kernel(
         for b in range(BATCH):
             nc.sync.dma_start(
                 out=out_2[b].rearrange("h l d -> l h d"),
-                in_=result[b * POSITIONS : (b + 1) * POSITIONS].rearrange("p h i r -> p h (i r)"),
+                in_=result[b:P:BATCH].rearrange("p h i r -> p h (i r)"),
             )

@@ -117,10 +117,10 @@ def tile_selfattention_pa_k_kernel(
         x_sb = []
         for chunk in range(X_CHUNKS):
             x_sb.append(keep.tile([P, x_cols], BF16, name="x_sb%d" % chunk))
-            for b in range(BATCH):
-                nc.sync.dma_start(
-                    out=x_sb[chunk][b:P:BATCH, :], in_=x[b, :, chunk * x_cols : (chunk + 1) * x_cols]
-                )
+            nc.sync.dma_start(
+                out=x_sb[chunk][:],
+                in_=x.rearrange("b l k -> (b l) k")[:, chunk * x_cols : (chunk + 1) * x_cols],
+            )
 
         planes = keep.tile([P, PASSES, COLS], U8, align_bytes=64)
         load_weight_scales(nc, planes, qkv_w_scales)
@@ -200,8 +200,8 @@ def tile_selfattention_pa_k_kernel(
                             ident_f32[:],
                         )
                 nc.scalar.copy(
-                    out=grouped[:, first : first + 2, :, :].bitcast(F32),
-                    in_=turned[:].rearrange("p g u m -> p g m u"),
+                    out=grouped[:, first : first + 2, :, :].bitcast(F32).rearrange("p g (l b) u -> p g l b u", b=BATCH),
+                    in_=turned[:].rearrange("p g u (b l) -> p g l b u", b=BATCH),
                 )
             done = slice(chunk * PASSES_PER_CHUNK * P, (chunk + 1) * PASSES_PER_CHUNK * P)
             nc.vector.quantize_mx(

@@ -35,7 +35,7 @@ GAIN_ROW = BIAS_ROWS
 X_CHUNKS = 4
 PASSES_PER_CHUNK = PASSES // X_CHUNKS
 SCALE_PASSES_PER_DMA = 4
-WORD_PASSES_PER_DMA = 2
+WORD_LOADS = [(0, 16, 2, 0, 1), (0, 16, 2, 1, 2), (0, 14, 2, 2, 3), (14, 16, 1, 2, 3)]
 
 FLOPS = 2 * P * K * COLS
 
@@ -52,33 +52,45 @@ def load_weight_scales(nc, planes, qkv_w_scales):
             )
 
 
-def load_weight_words(nc, words, qkv_w_words, stream):
-    some_bytes = slice(2 * STREAM * stream, 2 * STREAM * (stream + 1))
-    for n, first_pass in enumerate(range(0, PASSES, WORD_PASSES_PER_DMA)):
-        nc.sync.dma_start(
-            out=words[n][:].bitcast(I32),
-            in_=qkv_w_words[first_pass : first_pass + WORD_PASSES_PER_DMA, :, some_bytes]
-            .rearrange("g p c -> p g c")
-            .bitcast(I32),
-        )
-
-
-def multiply(nc, accs, x_codes, x_scales, words, planes, stream):
-    for g in range(PASSES):
-        tokens = slice(g * P, (g + 1) * P)
-        for j in range(BANKS_PER_STREAM):
-            first_col = STREAM * stream + BANK * j
-            nc.tensor.matmul_mx(
-                out=accs[j][:],
-                lhsT=x_codes[:, tokens].bitcast(FP8X4),
-                lhsT_scale=x_scales[:, tokens],
-                rhs=words[g // WORD_PASSES_PER_DMA][
-                    :, g % WORD_PASSES_PER_DMA, 2 * BANK * j : 2 * BANK * (j + 1)
-                ].bitcast(FP4X4),
-                rhs_scale=planes[:, g, first_col : first_col + BANK],
-                start=(g == 0),
-                stop=(g == PASSES - 1),
+def load_weight_words(nc, pool, qkv_w_words):
+    words = [[None] * PASSES for _ in range(STREAMS)]
+    for first_pass, last_pass, per_dma, first_stream, last_stream in WORD_LOADS:
+        first_byte = 2 * STREAM * first_stream
+        width = 2 * STREAM * (last_stream - first_stream)
+        for g in range(first_pass, last_pass, per_dma):
+            count = min(per_dma, last_pass - g)
+            tile = pool.tile(
+                [P, count, width], U8, name="words%d_%d" % (first_stream, g), align_bytes=64
             )
+            nc.sync.dma_start(
+                out=tile[:].bitcast(I32),
+                in_=qkv_w_words[g : g + count, :, first_byte : first_byte + width]
+                .rearrange("g p c -> p g c")
+                .bitcast(I32),
+            )
+            for i in range(count):
+                for stream in range(first_stream, last_stream):
+                    start = 2 * STREAM * (stream - first_stream)
+                    words[stream][g + i] = tile[:, i, start : start + 2 * STREAM]
+    return words
+
+
+def multiply(nc, accs, x_codes, x_scales, words, planes):
+    for first_pass, last_pass, per_dma, first_stream, last_stream in WORD_LOADS:
+        for g in range(first_pass, last_pass):
+            tokens = slice(g * P, (g + 1) * P)
+            for stream in range(first_stream, last_stream):
+                for j in range(BANKS_PER_STREAM):
+                    first_col = STREAM * stream + BANK * j
+                    nc.tensor.matmul_mx(
+                        out=accs[stream][j][:],
+                        lhsT=x_codes[:, tokens].bitcast(FP8X4),
+                        lhsT_scale=x_scales[:, tokens],
+                        rhs=words[stream][g][:, 2 * BANK * j : 2 * BANK * (j + 1)].bitcast(FP4X4),
+                        rhs_scale=planes[:, g, first_col : first_col + BANK],
+                        start=(g == 0),
+                        stop=(g == PASSES - 1),
+                    )
 
 
 def tile_selfattention_pa_k_kernel(
@@ -98,7 +110,7 @@ def tile_selfattention_pa_k_kernel(
 
         warm = keep.tile([P, 1], F32)
         nc.vector.memset(warm[:], 1.0)
-        nc.scalar.sqrt(warm[:], warm[:])
+        nc.scalar.activation(out=warm[:], in_=warm[:], func=ACT.Abs_reciprocal_sqrt)
         eps = keep.tile([P, 1], F32)
         nc.vector.memset(eps[:], EPS)
 
@@ -124,17 +136,7 @@ def tile_selfattention_pa_k_kernel(
 
         planes = keep.tile([P, PASSES, COLS], U8, align_bytes=64)
         load_weight_scales(nc, planes, qkv_w_scales)
-        words = []
-        for stream in range(STREAMS):
-            words.append(
-                [
-                    keep.tile(
-                        [P, WORD_PASSES_PER_DMA, 2 * STREAM], U8, name="words%d_%d" % (stream, n), align_bytes=64
-                    )
-                    for n in range(PASSES // WORD_PASSES_PER_DMA)
-                ]
-            )
-            load_weight_words(nc, words[stream], qkv_w_words, stream)
+        words = load_weight_words(nc, keep, qkv_w_words)
 
         bias_qk = keep.tile([P, 2, 2, HEADS, PAIRS], BF16)
         bias_v = keep.tile([P, STREAM], BF16)
@@ -210,33 +212,24 @@ def tile_selfattention_pa_k_kernel(
                 in_=grouped[:].rearrange("p g m t -> p (g m t)"),
             )
 
-        for stream, out_dram in enumerate((out_0, out_1)):
-            acc = [psum_acc.tile([P, BANK], F32, name="acc%d_%d" % (stream, j)) for j in range(BANKS_PER_STREAM)]
-            multiply(nc, acc, x_codes, x_scales, words[stream], planes, stream)
+        accs = [
+            [psum_acc.tile([P, BANK], F32, name="acc%d_%d" % (stream, j)) for j in range(BANKS_PER_STREAM)]
+            for stream in range(STREAMS)
+        ]
+        multiply(nc, accs, x_codes, x_scales, words, planes)
 
+        for stream, out_dram in enumerate((out_0, out_1)):
             y = stage.tile([P, 2, HEADS, PAIRS], F32)
+            squares = stage.tile([P, 2, HEADS, PAIRS], F32)
             for half in range(BANKS_PER_STREAM):
                 heads = slice(half * HEADS_PER_BANK, (half + 1) * HEADS_PER_BANK)
                 nc.vector.tensor_tensor(
                     out=y[:, :, heads, :],
-                    in0=acc[half][:].rearrange("p (h i c) -> p c h i", i=PAIRS, c=2),
+                    in0=accs[stream][half][:].rearrange("p (h i c) -> p c h i", i=PAIRS, c=2),
                     in1=bias_qk[:, stream, :, heads, :],
                     op=ALU.add,
                 )
-
-            squares = stage.tile([P, 2, HEADS, PAIRS], F32, bufs=1)
-            nc.scalar.square(squares[:], y[:])
-            sum_squares = stage.tile([P, HEADS], F32)
-            nc.vector.tensor_reduce(
-                out=sum_squares[:],
-                in_=squares[:].rearrange("p c h i -> p h c i"),
-                axis=mybir.AxisListType.XY,
-                op=ALU.add,
-            )
-            rms = stage.tile([P, HEADS], F32)
-            nc.scalar.activation(out=rms[:], in_=sum_squares[:], func=ACT.Sqrt, bias=eps[:], scale=1.0 / FEATURES)
-            inv_rms = stage.tile([P, HEADS], F32)
-            nc.vector.reciprocal(inv_rms[:], rms[:])
+                nc.scalar.square(squares[:, :, heads, :], y[:, :, heads, :])
 
             turned_y = stage.tile([P, 2, HEADS, PAIRS], F32)
             nc.vector.tensor_tensor(
@@ -245,39 +238,46 @@ def tile_selfattention_pa_k_kernel(
                 in1=coef_same[:, stream, :, :].unsqueeze(2).to_broadcast([P, 2, HEADS, PAIRS]),
                 op=ALU.mult,
             )
-            partner = stage.tile([P, 2, HEADS, PAIRS], F32, bufs=1)
-            for r in range(2):
-                nc.vector.tensor_tensor(
-                    out=partner[:, r, :, :],
-                    in0=y[:, 1 - r, :, :],
-                    in1=coef_other[:, stream, r, :].unsqueeze(1).to_broadcast([P, HEADS, PAIRS]),
-                    op=ALU.mult,
-                )
+
+            sum_squares = stage.tile([P, HEADS], F32)
+            nc.vector.tensor_reduce(
+                out=sum_squares[:],
+                in_=squares[:].rearrange("p c h i -> p h c i"),
+                axis=mybir.AxisListType.XY,
+                op=ALU.add,
+            )
+            inv_rms = stage.tile([P, HEADS], F32)
+            nc.scalar.activation(
+                out=inv_rms[:], in_=sum_squares[:], func=ACT.Abs_reciprocal_sqrt, bias=eps[:], scale=1.0 / FEATURES
+            )
+
+            partner = stage.tile([P, 2, HEADS, PAIRS], F32)
+            nc.vector.tensor_tensor(
+                out=partner[:],
+                in0=y[:, ::-1, :, :],
+                in1=coef_other[:, stream, :, :].unsqueeze(2).to_broadcast([P, 2, HEADS, PAIRS]),
+                op=ALU.mult,
+            )
             nc.vector.tensor_tensor(out=turned_y[:], in0=turned_y[:], in1=partner[:], op=ALU.add)
 
             result = stage.tile([P, HEADS, PAIRS, 2], F32, bufs=3)
-            nc.vector.tensor_tensor(
-                out=result[:],
-                in0=turned_y[:].rearrange("p r h i -> p h i r"),
-                in1=inv_rms[:].unsqueeze(2).unsqueeze(3).to_broadcast([P, HEADS, PAIRS, 2]),
-                op=ALU.mult,
-            )
+            for h in range(HEADS):
+                nc.scalar.mul(
+                    result[:, h, :, :], turned_y[:, :, h, :].rearrange("p r i -> p i r"), inv_rms[:, h : h + 1]
+                )
             for b in range(BATCH):
                 nc.sync.dma_start(
                     out=out_dram[b].rearrange("h l d -> l h d"),
                     in_=result[b:P:BATCH].rearrange("p h i r -> p h (i r)"),
                 )
 
-        acc_v = [psum_acc.tile([P, BANK], F32, name="acc_v%d" % j) for j in range(BANKS_PER_STREAM)]
-        multiply(nc, acc_v, x_codes, x_scales, words[2], planes, 2)
-
-        result = stage.tile([P, HEADS, PAIRS, 2], F32, bufs=3)
-        result_v = result[:].rearrange("p h i r -> p (h i r)")
         for j in range(BANKS_PER_STREAM):
-            cols = slice(j * BANK, (j + 1) * BANK)
-            nc.vector.tensor_tensor(out=result_v[:, cols], in0=acc_v[j][:], in1=bias_v[:, cols], op=ALU.add)
-        for b in range(BATCH):
-            nc.sync.dma_start(
-                out=out_2[b].rearrange("h l d -> l h d"),
-                in_=result[b:P:BATCH].rearrange("p h i r -> p h (i r)"),
+            result_v = stage.tile([P, BANK], F32)
+            nc.vector.tensor_tensor(
+                out=result_v[:], in0=accs[2][j][:], in1=bias_v[:, j * BANK : (j + 1) * BANK], op=ALU.add
             )
+            for b in range(BATCH):
+                nc.sync.dma_start(
+                    out=out_2[b, j * HEADS_PER_BANK : (j + 1) * HEADS_PER_BANK].rearrange("h l d -> l h d"),
+                    in_=result_v[b:P:BATCH].rearrange("p (h d) -> p h d", d=FEATURES),
+                )

@@ -260,16 +260,20 @@ def tile_selfattention_pa_k_kernel(
             )
             nc.vector.tensor_tensor(out=turned_y[:], in0=turned_y[:], in1=partner[:], op=ALU.add)
 
-            result = stage.tile([P, HEADS, PAIRS, 2], F32, bufs=3)
-            for h in range(HEADS):
-                nc.scalar.mul(
-                    result[:, h, :, :], turned_y[:, :, h, :].rearrange("p r i -> p i r"), inv_rms[:, h : h + 1]
+            for half in range(BANKS_PER_STREAM):
+                heads = slice(half * HEADS_PER_BANK, (half + 1) * HEADS_PER_BANK)
+                result = stage.tile([P, HEADS_PER_BANK, PAIRS, 2], F32, bufs=4)
+                nc.vector.tensor_tensor(
+                    out=result[:],
+                    in0=turned_y[:, :, heads, :].rearrange("p r h i -> p h i r"),
+                    in1=inv_rms[:, heads].unsqueeze(2).unsqueeze(3).to_broadcast([P, HEADS_PER_BANK, PAIRS, 2]),
+                    op=ALU.mult,
                 )
-            for b in range(BATCH):
-                nc.sync.dma_start(
-                    out=out_dram[b].rearrange("h l d -> l h d"),
-                    in_=result[b:P:BATCH].rearrange("p h i r -> p h (i r)"),
-                )
+                for b in range(BATCH):
+                    nc.sync.dma_start(
+                        out=out_dram[b, heads].rearrange("h l d -> l h d"),
+                        in_=result[b:P:BATCH].rearrange("p h i r -> p h (i r)"),
+                    )
 
         for j in range(BANKS_PER_STREAM):
             result_v = stage.tile([P, BANK], F32)

from contextlib import ExitStack

import concourse.mybir as mybir
from concourse.masks import make_identity

F32 = mybir.dt.float32
BF16 = mybir.dt.bfloat16
I32 = mybir.dt.int32
U8 = mybir.dt.uint8
U32 = mybir.dt.uint32
FP8X4 = mybir.dt.float8_e4m3fn_x4
FP4X4 = mybir.dt.float4_e2m1fn_x4
ALU = mybir.AluOpType
ACT = mybir.ActivationFunctionType

P = 128
BATCH = 2
K = 8192
K_PASS = 512
PASSES = K // K_PASS
HEADS = 16
FEATURES = 64
PAIRS = FEATURES // 2
STREAM = HEADS * FEATURES
BANK = 512
HEADS_PER_BANK = BANK // FEATURES
EPS = 1e-6

STREAMS = 3
COLS = STREAMS * STREAM
BANKS_PER_STREAM = STREAM // BANK
BIAS_ROWS = COLS // BANK
GAIN_ROW = BIAS_ROWS

X_CHUNKS = 4
PASSES_PER_CHUNK = PASSES // X_CHUNKS
SCALE_PASSES_PER_DMA = 4
WORD_LOADS = [(0, 16, 2, 0, 1), (0, 16, 2, 1, 2), (0, 14, 2, 2, 3), (14, 16, 1, 2, 3)]

FLOPS = 2 * P * K * COLS


def load_weight_scales(nc, planes, qkv_w_scales):
    for first_pass in range(0, PASSES, SCALE_PASSES_PER_DMA):
        some = slice(first_pass, first_pass + SCALE_PASSES_PER_DMA)
        nc.vector.memset(planes[:, some, :].bitcast(I32), 0)
        for q in range(8):
            partition = 32 * (q // 4) + q % 4
            nc.sync.dma_start(
                out=planes[partition:P:64, some, :].bitcast(I32),
                in_=qkv_w_scales[some, q:16:8, :].rearrange("g q n -> q g n").bitcast(I32),
            )


def load_weight_words(nc, pool, qkv_w_words):
    words = [[None] * PASSES for _ in range(STREAMS)]
    for first_pass, last_pass, per_dma, first_stream, last_stream in WORD_LOADS:
        first_byte = 2 * STREAM * first_stream
        width = 2 * STREAM * (last_stream - first_stream)
        for g in range(first_pass, last_pass, per_dma):
            count = min(per_dma, last_pass - g)
            tile = pool.tile(
                [P, count, width], U8, name="words%d_%d" % (first_stream, g), align_bytes=64
            )
            nc.sync.dma_start(
                out=tile[:].bitcast(I32),
                in_=qkv_w_words[g : g + count, :, first_byte : first_byte + width]
                .rearrange("g p c -> p g c")
                .bitcast(I32),
            )
            for i in range(count):
                for stream in range(first_stream, last_stream):
                    start = 2 * STREAM * (stream - first_stream)
                    words[stream][g + i] = tile[:, i, start : start + 2 * STREAM]
    return words


def multiply(nc, accs, x_codes, x_scales, words, planes):
    for first_pass, last_pass, per_dma, first_stream, last_stream in WORD_LOADS:
        for g in range(first_pass, last_pass):
            tokens = slice(g * P, (g + 1) * P)
            for stream in range(first_stream, last_stream):
                for j in range(BANKS_PER_STREAM):
                    first_col = STREAM * stream + BANK * j
                    nc.tensor.matmul_mx(
                        out=accs[stream][j][:],
                        lhsT=x_codes[:, tokens].bitcast(FP8X4),
                        lhsT_scale=x_scales[:, tokens],
                        rhs=words[stream][g][:, 2 * BANK * j : 2 * BANK * (j + 1)].bitcast(FP4X4),
                        rhs_scale=planes[:, g, first_col : first_col + BANK],
                        start=(g == 0),
                        stop=(g == PASSES - 1),
                    )


def tile_selfattention_pa_k_kernel(
    tc, x, pe, qkv_w_words, qkv_w_scales, qkv_b, q_scale, k_scale, out_0, out_1, out_2
):
    nc = tc.nc
    with ExitStack() as ctx:
        keep = ctx.enter_context(tc.tile_pool(name="keep", bufs=1))
        stage = ctx.enter_context(tc.tile_pool(name="stage", bufs=2))
        psum_acc = ctx.enter_context(tc.psum_pool(name="psum_acc", bufs=1))
        psum_tmp = ctx.enter_context(tc.psum_pool(name="psum_tmp", bufs=2))

        ident_f32 = keep.tile([P, P], F32)
        make_identity(nc, ident_f32[:])
        ident_bf16 = keep.tile([P, P], BF16)
        make_identity(nc, ident_bf16[:])

        warm = keep.tile([P, 1], F32)
        nc.vector.memset(warm[:], 1.0)
        nc.scalar.activation(out=warm[:], in_=warm[:], func=ACT.Abs_reciprocal_sqrt)
        eps = keep.tile([P, 1], F32)
        nc.vector.memset(eps[:], EPS)

        vectors = keep.tile([P, BANK], BF16)
        nc.vector.memset(vectors[:], 0.0)
        nc.scalar.dma_start(out=vectors[0:BIAS_ROWS, :], in_=qkv_b.rearrange("(j n) -> j n", n=BANK))
        nc.scalar.dma_start(out=vectors[GAIN_ROW : GAIN_ROW + 1, 0:FEATURES], in_=q_scale.unsqueeze(0))
        nc.scalar.dma_start(
            out=vectors[GAIN_ROW : GAIN_ROW + 1, FEATURES : 2 * FEATURES], in_=k_scale.unsqueeze(0)
        )
        pe_sb = keep.tile([P, PAIRS, 2, 2], BF16)
        for b in range(BATCH):
            nc.scalar.dma_start(out=pe_sb[b:P:BATCH], in_=pe.rearrange("a b l i r c -> (a b l) i r c"))

        x_cols = K // X_CHUNKS
        x_sb = []
        for chunk in range(X_CHUNKS):
            x_sb.append(keep.tile([P, x_cols], BF16, name="x_sb%d" % chunk))
            nc.sync.dma_start(
                out=x_sb[chunk][:],
                in_=x.rearrange("b l k -> (b l) k")[:, chunk * x_cols : (chunk + 1) * x_cols],
            )

        planes = keep.tile([P, PASSES, COLS], U8, align_bytes=64)
        load_weight_scales(nc, planes, qkv_w_scales)
        words = load_weight_words(nc, keep, qkv_w_words)

        bias_qk = keep.tile([P, 2, 2, HEADS, PAIRS], BF16)
        bias_v = keep.tile([P, STREAM], BF16)
        for j in range(BIAS_ROWS):
            spread = psum_tmp.tile([P, BANK], F32, tag="tmp")
            nc.tensor.matmul(
                out=spread[:],
                lhsT=ident_bf16[:, j : j + 1].to_broadcast([P, P]),
                rhs=vectors[:],
                start=True,
                stop=True,
            )
            stream = j // BANKS_PER_STREAM
            half = j % BANKS_PER_STREAM
            if stream < 2:
                heads = slice(half * HEADS_PER_BANK, (half + 1) * HEADS_PER_BANK)
                nc.scalar.copy(
                    out=bias_qk[:, stream, :, heads, :],
                    in_=spread[:].rearrange("p (h i c) -> p c h i", i=PAIRS, c=2),
                )
            else:
                nc.scalar.copy(out=bias_v[:, half * BANK : (half + 1) * BANK], in_=spread[:])

        gains = psum_tmp.tile([P, BANK], F32, tag="tmp")
        nc.tensor.matmul(
            out=gains[:],
            lhsT=ident_bf16[:, GAIN_ROW : GAIN_ROW + 1].to_broadcast([P, P]),
            rhs=vectors[:],
            start=True,
            stop=True,
        )
        gain = gains[:, 0 : 2 * FEATURES].rearrange("p (s i c) -> p s i c", s=2, c=2)

        coef_same = keep.tile([P, 2, 2, PAIRS], F32)
        coef_other = keep.tile([P, 2, 2, PAIRS], F32)
        for r in range(2):
            nc.vector.tensor_tensor(
                out=coef_same[:, :, r, :],
                in0=gain[:, :, :, r],
                in1=pe_sb[:, :, r, r].unsqueeze(1).to_broadcast([P, 2, PAIRS]),
                op=ALU.mult,
            )
            nc.vector.tensor_tensor(
                out=coef_other[:, :, r, :],
                in0=gain[:, :, :, 1 - r],
                in1=pe_sb[:, :, r, 1 - r].unsqueeze(1).to_broadcast([P, 2, PAIRS]),
                op=ALU.mult,
            )

        x_codes = keep.tile([P, PASSES * P], U32, align_bytes=64)
        x_scales = keep.tile([P, PASSES * P], U8, align_bytes=64)
        for chunk in range(X_CHUNKS):
            x_words = x_sb[chunk][:].bitcast(F32)
            grouped = stage.tile([P, PASSES_PER_CHUNK, P, 4], BF16, align_bytes=64)
            for first in range(0, PASSES_PER_CHUNK, 2):
                turned = psum_tmp.tile([P, 2, 2, P], F32, tag="tmp")
                for g in range(2):
                    for u in range(2):
                        start_col = (K_PASS // 2) * (first + g)
                        nc.tensor.transpose(
                            turned[:, g, u, :],
                            x_words[:, start_col + u : start_col + K_PASS // 2 : 2],
                            ident_f32[:],
                        )
                nc.scalar.copy(
                    out=grouped[:, first : first + 2, :, :].bitcast(F32).rearrange("p g (l b) u -> p g l b u", b=BATCH),
                    in_=turned[:].rearrange("p g u (b l) -> p g l b u", b=BATCH),
                )
            done = slice(chunk * PASSES_PER_CHUNK * P, (chunk + 1) * PASSES_PER_CHUNK * P)
            nc.vector.quantize_mx(
                out=x_codes[:, done].bitcast(FP8X4),
                scales=x_scales[:, done],
                in_=grouped[:].rearrange("p g m t -> p (g m t)"),
            )

        accs = [
            [psum_acc.tile([P, BANK], F32, name="acc%d_%d" % (stream, j)) for j in range(BANKS_PER_STREAM)]
            for stream in range(STREAMS)
        ]
        multiply(nc, accs, x_codes, x_scales, words, planes)

        for stream, out_dram in enumerate((out_0, out_1)):
            y = stage.tile([P, 2, HEADS, PAIRS], F32)
            squares = stage.tile([P, 2, HEADS, PAIRS], F32)
            for half in range(BANKS_PER_STREAM):
                heads = slice(half * HEADS_PER_BANK, (half + 1) * HEADS_PER_BANK)
                nc.vector.tensor_tensor(
                    out=y[:, :, heads, :],
                    in0=accs[stream][half][:].rearrange("p (h i c) -> p c h i", i=PAIRS, c=2),
                    in1=bias_qk[:, stream, :, heads, :],
                    op=ALU.add,
                )
                nc.scalar.square(squares[:, :, heads, :], y[:, :, heads, :])

            turned_y = stage.tile([P, 2, HEADS, PAIRS], F32)
            nc.vector.tensor_tensor(
                out=turned_y[:],
                in0=y[:],
                in1=coef_same[:, stream, :, :].unsqueeze(2).to_broadcast([P, 2, HEADS, PAIRS]),
                op=ALU.mult,
            )

            sum_squares = stage.tile([P, HEADS], F32)
            nc.vector.tensor_reduce(
                out=sum_squares[:],
                in_=squares[:].rearrange("p c h i -> p h c i"),
                axis=mybir.AxisListType.XY,
                op=ALU.add,
            )
            inv_rms = stage.tile([P, HEADS], F32)
            nc.scalar.activation(
                out=inv_rms[:], in_=sum_squares[:], func=ACT.Abs_reciprocal_sqrt, bias=eps[:], scale=1.0 / FEATURES
            )

            partner = stage.tile([P, 2, HEADS, PAIRS], F32)
            nc.vector.tensor_tensor(
                out=partner[:],
                in0=y[:, ::-1, :, :],
                in1=coef_other[:, stream, :, :].unsqueeze(2).to_broadcast([P, 2, HEADS, PAIRS]),
                op=ALU.mult,
            )
            nc.vector.tensor_tensor(out=turned_y[:], in0=turned_y[:], in1=partner[:], op=ALU.add)

            for half in range(BANKS_PER_STREAM):
                heads = slice(half * HEADS_PER_BANK, (half + 1) * HEADS_PER_BANK)
                result = stage.tile([P, HEADS_PER_BANK, PAIRS, 2], F32, bufs=4)
                nc.vector.tensor_tensor(
                    out=result[:],
                    in0=turned_y[:, :, heads, :].rearrange("p r h i -> p h i r"),
                    in1=inv_rms[:, heads].unsqueeze(2).unsqueeze(3).to_broadcast([P, HEADS_PER_BANK, PAIRS, 2]),
                    op=ALU.mult,
                )
                for b in range(BATCH):
                    nc.sync.dma_start(
                        out=out_dram[b, heads].rearrange("h l d -> l h d"),
                        in_=result[b:P:BATCH].rearrange("p h i r -> p h (i r)"),
                    )

        for j in range(BANKS_PER_STREAM):
            result_v = stage.tile([P, BANK], F32)
            nc.vector.tensor_tensor(
                out=result_v[:], in0=accs[2][j][:], in1=bias_v[:, j * BANK : (j + 1) * BANK], op=ALU.add
            )
            for b in range(BATCH):
                nc.sync.dma_start(
                    out=out_2[b, j * HEADS_PER_BANK : (j + 1) * HEADS_PER_BANK].rearrange("h l d -> l h d"),
                    in_=result_v[b:P:BATCH].rearrange("p (h d) -> p h d", d=FEATURES),
                )
